import numpy as np
import ml_dtypes


def mxq(x, axis, fmt="e4m3"):
    dtype, down = {"e4m3": (ml_dtypes.float8_e4m3fn, 7), "e5m2": (ml_dtypes.float8_e5m2, 14)}[fmt]
    v = np.moveaxis(np.asarray(x, np.float32).astype(ml_dtypes.bfloat16).astype(np.float64), axis, -1)
    blocks = v.reshape(v.shape[:-1] + (-1, 32))
    amax = np.abs(blocks).max(-1, keepdims=True)
    byte = np.maximum(np.where(amax > 0, np.frexp(amax)[1] - 1 + 127, 0) - down, 1)
    scale = np.exp2(byte - 127.0)
    codes = (blocks / scale).astype(np.float32).astype(dtype).astype(np.float64)
    return np.moveaxis((codes * scale).reshape(v.shape), -1, axis)


WIDE = False


def mx_kscale(k):
    if not WIDE:
        return np.ones(k)
    levels = np.array([30, -30])
    if k % 512:
        return np.exp2(np.random.permutation(np.resize(levels, k // 32))).repeat(32)
    a = np.empty((k // 512, 16))
    for p in range(k // 512):
        a[p, :8] = np.random.permutation(np.resize(levels, 8))
        for g in range(8):
            far = levels[np.abs(levels - a[p, g]) >= 10]
            a[p, g + 8] = far[np.random.randint(len(far))]
    return np.exp2(a.ravel()).repeat(32)


BF16 = ml_dtypes.bfloat16


def bf(x):
    return np.asarray(x, np.float32).astype(BF16)


def f64(x):
    return np.asarray(x).astype(np.float64)


E2M1 = np.array([0.0, 0.5, 1.0, 1.5, 2.0, 3.0, 4.0, 6.0, -0.0, -0.5, -1.0, -1.5, -2.0, -3.0, -4.0, -6.0])


def pack_weight(w, fmt):
    k, n = w.shape
    w = f64(bf(w)).reshape(k // 32, 32, n)
    amax = np.abs(w).max(1)
    if fmt == "e4m3":
        byte = np.frexp(amax)[1] - 1 + 127 - 7
    else:
        mant, ex = np.frexp(amax / 6.0)
        byte = np.where(mant > 0.5, ex, ex - 1) + 127
    byte = np.clip(np.where(amax > 0, byte, 1), 1, 254)
    scaled = (w * np.exp2(127.0 - byte)[:, None, :]).reshape(k, n).astype(np.float32)
    by_word = np.ascontiguousarray(scaled.reshape(k // 512, 128, 4, n).transpose(0, 1, 3, 2))
    if fmt == "e4m3":
        words = by_word.astype(ml_dtypes.float8_e4m3fn).view(np.uint8)
    else:
        c = by_word.astype(ml_dtypes.float4_e2m1fn).view(np.uint8) & 0xF
        words = c[..., 0::2] | (c[..., 1::2] << 4)
    return np.ascontiguousarray(words), np.ascontiguousarray(byte.astype(np.uint8).reshape(k // 512, 16, n))


def unpack_weight(words, scales, fmt):
    g, p, n, _ = words.shape
    if fmt == "e4m3":
        vals = np.ascontiguousarray(words).view(ml_dtypes.float8_e4m3fn).astype(np.float64)
    else:
        nib = np.empty((g, p, n, 4), np.uint8)
        nib[..., 0::2] = words & 0xF
        nib[..., 1::2] = words >> 4
        vals = E2M1[nib]
    vals = vals * np.repeat(np.exp2(scales.astype(np.float64) - 127.0), 8, axis=1)[..., None]
    return vals.transpose(0, 1, 3, 2).reshape(g * 512, n)

def pack4(w):
    words, scales = pack_weight(w, "e2m1")
    return words.reshape(words.shape[0], 128, -1), scales


def unpack4(words, scales):
    return unpack_weight(words.reshape(words.shape[0], 128, -1, 2), scales, "e2m1")


H, D_CONTENT, D_POS, D_K, D_V, B, L = 8, 768, 256, 128, 128, 4, 256
D_MODEL = D_CONTENT + D_POS
T = B * L
DV1 = D_V // 2
KP = H * DV1
EPS = 1e-3


def setup_inputs():
    s1, s2 = mx_kscale(KP), mx_kscale(KP)
    sc = np.concatenate([s1.reshape(H, DV1), s2.reshape(H, DV1)], axis=1)
    attn_out = bf(np.random.standard_normal((H, B, L, D_V)) * 0.4 * sc[:, None, None, :])
    inp = bf(np.random.standard_normal((T, D_MODEL)) * 0.05 + np.random.standard_normal((T, 1)) * 0.03)
    w_proj1_words, w_proj1_scales = pack4(np.random.standard_normal((KP, D_CONTENT)) * 0.1 / np.sqrt(KP) / s1[:, None])
    w_proj2_words, w_proj2_scales = pack4(np.random.standard_normal((KP, D_POS)) * 0.1 / np.sqrt(KP) / s2[:, None])
    ln_a = bf(1.0 + 0.1 * np.random.standard_normal(D_MODEL))
    ln_b = bf(0.1 * np.random.standard_normal(D_MODEL))
    return {
        "attn_out": attn_out,
        "inp": inp,
        "w_proj1_words": w_proj1_words,
        "w_proj1_scales": w_proj1_scales,
        "w_proj2_words": w_proj2_words,
        "w_proj2_scales": w_proj2_scales,
        "ln_a": ln_a,
        "ln_b": ln_b,
    }


def reference(attn_out, inp, w_proj1_words, w_proj1_scales, w_proj2_words, w_proj2_scales, ln_a, ln_b):
    o = f64(attn_out).reshape(H, T, D_V).transpose(1, 0, 2)
    o1 = o[:, :, :DV1].reshape(T, KP)
    o2 = o[:, :, DV1:].reshape(T, KP)
    y1 = mxq(o1, 1, "e5m2") @ unpack4(w_proj1_words, w_proj1_scales)
    y2 = mxq(o2, 1, "e5m2") @ unpack4(w_proj2_words, w_proj2_scales)
    z = np.concatenate([y1, y2], -1) + f64(inp)
    mu = np.mean(z, axis=-1, keepdims=True)
    sigma = np.std(z, axis=-1, keepdims=True, ddof=1)
    ln = (z - mu) / (sigma + EPS)
    return ln * f64(ln_a) + f64(ln_b)

@@ -1,0 +1,232 @@
+from contextlib import ExitStack
+
+import concourse.mybir as mybir
+from concourse.masks import make_identity
+
+H, D_CONTENT, D_POS, D_V, T = 8, 768, 256, 128, 1024
+D_MODEL = D_CONTENT + D_POS
+HALF = D_V // 2
+K = H * HALF
+EPS = 1e-3
+FLOPS = 2 * T * K * D_MODEL
+
+P = 128
+TILES = T // P
+BANK = 512
+
+F32 = mybir.dt.float32
+BF16 = mybir.dt.bfloat16
+I32 = mybir.dt.int32
+U32 = mybir.dt.uint32
+U8 = mybir.dt.uint8
+E5M2X4 = mybir.dt.float8_e5m2_x4
+E2M1X4 = mybir.dt.float4_e2m1fn_x4
+ALU = mybir.AluOpType
+ACT = mybir.ActivationFunctionType
+
+SUM_LO, SUM_HI, NEG_MEAN, SUM_SQ, SIGMA, DENOM, RSTD = range(7)
+
+
+def tile_multiheadattention_pa_kernel(
+    tc, attn_out, inp, w_proj1_words, w_proj1_scales, w_proj2_words, w_proj2_scales, ln_a, ln_b, out
+):
+    nc = tc.nc
+    heads = attn_out.rearrange("h b l d -> (b l) h d")
+
+    with ExitStack() as ctx:
+        const = ctx.enter_context(tc.tile_pool(name="const", bufs=1))
+        work = ctx.enter_context(tc.tile_pool(name="work", bufs=TILES))
+        psum_const = ctx.enter_context(tc.psum_pool(name="psum_const", bufs=1))
+        psum = ctx.enter_context(tc.psum_pool(name="psum", bufs=2))
+        ctx.enter_context(tc.manual_schedule())
+
+        ident = const.tile([P, P], F32, name="ident")
+        row_select = const.tile([P, 2], BF16, name="row_select")
+        ab_rows = const.tile([P, D_MODEL], BF16, name="ab_rows")
+        bias_sb = const.tile([P, D_MODEL], BF16, name="bias_sb")
+        squares = const.tile([P, D_MODEL], F32, name="squares")
+        w1_codes = const.tile([P, 2 * D_CONTENT], U8, name="w1_codes", align_bytes=64)
+        w2_codes = const.tile([P, 2 * D_POS], U8, name="w2_codes", align_bytes=64)
+        w1_scale = const.tile([P, D_CONTENT], U8, name="w1_scale", align_bytes=64)
+        w2_scale = const.tile([P, D_POS], U8, name="w2_scale", align_bytes=64)
+        gain_ps = psum_const.tile([P, D_MODEL], BF16, name="gain_ps")
+        bias_ps = psum_const.tile([P, D_MODEL], BF16, name="bias_ps")
+
+        x = [work.tile([P, 2, H, HALF], BF16, name="x") for i in range(TILES)]
+        res = [work.tile([P, D_MODEL], BF16, name="res") for i in range(TILES)]
+        grouped = [work.tile([P, 2 * K], BF16, name="grouped", align_bytes=64) for i in range(TILES)]
+        codes = [work.tile([P, 2 * P], U32, name="codes", align_bytes=64) for i in range(TILES)]
+        scales = [work.tile([P, 2 * P], U8, name="scales", align_bytes=64) for i in range(TILES)]
+        z = [work.tile([P, D_MODEL], F32, name="z") for i in range(TILES)]
+        t = [work.tile([P, D_MODEL], F32, name="t") for i in range(TILES)]
+        stats = [work.tile([P, 8], F32, name="stats") for i in range(TILES)]
+        xt, y_lo, y_hi = {}, {}, {}
+
+        def rows(i):
+            return slice(i * P, (i + 1) * P)
+
+        def stat(i, col):
+            return stats[i][:, col : col + 1]
+
+        def load_half(i, s):
+            nc.sync.dma_start(out=x[i][:, s, :, :], in_=heads[rows(i), :, s * HALF : (s + 1) * HALF])
+
+        def load_res(i):
+            nc.sync.dma_start(out=res[i][:], in_=inp[rows(i), :])
+
+        def load_scales(plane, w_scales):
+            for q in range(4):
+                nc.sync.dma_start(
+                    out=plane[32 * q : 32 * q + 4, :].bitcast(I32),
+                    in_=w_scales[0, 4 * q : 4 * q + 4, :].bitcast(I32),
+                )
+
+        def spread_row(dst, row):
+            for n0 in range(0, D_MODEL, BANK):
+                nc.tensor.matmul(
+                    dst[:, n0 : n0 + BANK],
+                    lhsT=row_select[:, row : row + 1].to_broadcast([P, P]),
+                    rhs=ab_rows[:, n0 : n0 + BANK],
+                    start=True,
+                    stop=True,
+                )
+
+        def transpose(i):
+            xt[i] = psum.tile([P, 4, P], F32, name="xt")
+            words = x[i][:].rearrange("p s h j -> p (s h j)").bitcast(F32)
+            for s in range(2):
+                for u in range(2):
+                    nc.tensor.transpose(xt[i][:, 2 * s + u, :], words[:, 256 * s + u : 256 * (s + 1) : 2], ident[:])
+
+        def interleave(i):
+            nc.scalar.copy(
+                out=grouped[i][:].bitcast(F32).rearrange("p (s r u) -> p s r u", s=2, u=2),
+                in_=xt[i][:].rearrange("p (s u) r -> p s r u", s=2),
+            )
+
+        def quantize(i):
+            nc.vector.quantize_mx(out=codes[i][:].bitcast(E5M2X4), scales=scales[i][:], in_=grouped[i][:])
+
+        def project(i):
+            y_lo[i] = psum.tile([P, BANK], F32, name="y_lo")
+            y_hi[i] = psum.tile([P, BANK], F32, name="y_hi")
+            parts = (
+                (y_lo[i][:], 0, w1_codes, w1_scale, 0, BANK),
+                (y_hi[i][:, : D_CONTENT - BANK], 0, w1_codes, w1_scale, BANK, D_CONTENT),
+                (y_hi[i][:, D_CONTENT - BANK :], 1, w2_codes, w2_scale, 0, D_POS),
+            )
+            for dst, s, w_codes, w_scale, n0, n1 in parts:
+                nc.tensor.matmul_mx(
+                    out=dst,
+                    lhsT=codes[i][:, s * P : (s + 1) * P].bitcast(E5M2X4),
+                    lhsT_scale=scales[i][:, s * P : (s + 1) * P],
+                    rhs=w_codes[:, 2 * n0 : 2 * n1].bitcast(E2M1X4),
+                    rhs_scale=w_scale[:, n0:n1],
+                    start=True,
+                    stop=True,
+                )
+
+        def add_residual(i, y, n0, col):
+            cols = slice(n0, n0 + BANK)
+            nc.vector.scalar_tensor_tensor(
+                out=z[i][:, cols], in0=y[:], scalar=1.0, in1=res[i][:, cols],
+                op0=ALU.mult, op1=ALU.add, accum_out=stat(i, col),
+            )
+
+        def neg_mean(i):
+            nc.vector.tensor_scalar(
+                out=stat(i, NEG_MEAN), in0=stat(i, SUM_LO), scalar1=stat(i, SUM_HI), scalar2=-1.0 / D_MODEL,
+                op0=ALU.add, op1=ALU.mult,
+            )
+
+        def deviation(i):
+            nc.scalar.activation(
+                out=squares[:], in_=z[i][:], func=ACT.Square, bias=stat(i, NEG_MEAN), accum_out=stat(i, SUM_SQ)
+            )
+            nc.scalar.activation(out=stat(i, SIGMA), in_=stat(i, SUM_SQ), func=ACT.Sqrt, scale=1.0 / (D_MODEL - 1))
+            nc.scalar.activation(out=stat(i, DENOM), in_=stat(i, SIGMA), func=ACT.Copy, bias=EPS)
+
+        def centre_and_gain(i):
+            nc.vector.scalar_tensor_tensor(
+                out=t[i][:], in0=z[i][:], scalar=stat(i, NEG_MEAN), in1=gain_ps[:], op0=ALU.add, op1=ALU.mult
+            )
+
+        def reciprocal(i):
+            nc.vector.reciprocal(out=stat(i, RSTD), in_=stat(i, DENOM))
+
+        def finish(i):
+            nc.scalar.activation(out=t[i][:], in_=t[i][:], func=ACT.Copy, scale=stat(i, RSTD))
+            nc.gpsimd.tensor_tensor(out=t[i][:], in0=t[i][:], in1=bias_sb[:], op=ALU.add)
+            nc.sync.dma_start(out=out[rows(i), :], in_=t[i][:])
+
+        def finish_last(i):
+            for n0 in range(0, D_MODEL, BANK):
+                cols = slice(n0, n0 + BANK)
+                nc.vector.scalar_tensor_tensor(
+                    out=t[i][:, cols], in0=t[i][:, cols], scalar=stat(i, RSTD), in1=bias_ps[:, cols],
+                    op0=ALU.mult, op1=ALU.add,
+                )
+                nc.sync.dma_start(out=out[rows(i), cols], in_=t[i][:, cols])
+
+        nc.vector.memset(w1_scale[:].bitcast(I32), 0)
+        nc.vector.memset(w2_scale[:].bitcast(I32), 0)
+        nc.vector.memset(ab_rows[:].bitcast(I32), 0)
+        make_identity(nc, ident[:])
+        nc.scalar.activation(out=row_select[:], in_=ident[:, 0:2], func=ACT.Sqrt)
+
+        load_half(0, 0)
+        load_half(0, 1)
+        load_scales(w1_scale, w_proj1_scales)
+        load_half(1, 0)
+        load_half(1, 1)
+        load_res(0)
+        load_half(2, 0)
+        load_scales(w2_scale, w_proj2_scales)
+        load_half(2, 1)
+        load_res(1)
+        for i in range(3, TILES):
+            load_half(i, 0)
+            load_half(i, 1)
+            load_res(i - 1)
+        load_res(TILES - 1)
+        nc.gpsimd.dma_start(out=w1_codes[:].bitcast(I32), in_=w_proj1_words[0].bitcast(I32))
+        nc.gpsimd.dma_start(out=w2_codes[:].bitcast(I32), in_=w_proj2_words[0].bitcast(I32))
+        nc.gpsimd.dma_start(out=ab_rows[0:1, :], in_=ln_a.rearrange("(o n) -> o n", o=1))
+        nc.gpsimd.dma_start(out=ab_rows[1:2, :], in_=ln_b.rearrange("(o n) -> o n", o=1))
+
+        transpose(0)
+        interleave(0)
+        transpose(1)
+        interleave(1)
+        quantize(0)
+        project(0)
+        quantize(1)
+        transpose(2)
+        interleave(2)
+        project(1)
+        add_residual(0, y_lo[0], 0, SUM_LO)
+        spread_row(gain_ps, 0)
+
+        for i in range(TILES):
+            add_residual(i, y_hi[i], BANK, SUM_HI)
+            if i + 3 < TILES:
+                transpose(i + 3)
+            if i == 0:
+                spread_row(bias_ps, 1)
+            if i + 2 < TILES:
+                quantize(i + 2)
+                project(i + 2)
+            neg_mean(i)
+            if i + 1 < TILES:
+                add_residual(i + 1, y_lo[i + 1], 0, SUM_LO)
+            deviation(i)
+            centre_and_gain(i)
+            reciprocal(i)
+            if i + 3 < TILES:
+                interleave(i + 3)
+            if i == 0:
+                nc.scalar.copy(out=bias_sb[:], in_=bias_ps[:])
+            if i + 1 < TILES:
+                finish(i)
+            else:
+                finish_last(i)

@@ -13,6 +13,8 @@ FLOPS = 2 * T * K * D_MODEL
 P = 128
 TILES = T // P
 BANK = 512
+GROUPS = ((0,), (1,), (2, 3), (4, 5), (6, 7))
+LAG = 3
 
 F32 = mybir.dt.float32
 BF16 = mybir.dt.bfloat16
@@ -24,18 +26,23 @@ E2M1X4 = mybir.dt.float4_e2m1fn_x4
 ALU = mybir.AluOpType
 ACT = mybir.ActivationFunctionType
 
-SUM_LO, SUM_HI, NEG_MEAN, SUM_SQ, SIGMA, DENOM, RSTD = range(7)
+SUM_LO, SUM_HI, NEG_MEAN, SUM_SQ, EPS_SQ, ROOTS, DENOM, RSTD = 0, 1, 2, 3, 4, 5, 7, 8
+STAT_COLS = 9
+LO, HI, ALL = slice(0, BANK), slice(BANK, D_MODEL), slice(0, D_MODEL)
 
 
 def tile_multiheadattention_pa_kernel(
     tc, attn_out, inp, w_proj1_words, w_proj1_scales, w_proj2_words, w_proj2_scales, ln_a, ln_b, out
 ):
     nc = tc.nc
-    heads = attn_out.rearrange("h b l d -> (b l) h d")
+    heads = attn_out.rearrange("h b l d -> h (b l) d")
+    group_of = {i: g for g, tiles in enumerate(GROUPS) for i in tiles}
+    last = TILES - 1
 
     with ExitStack() as ctx:
         const = ctx.enter_context(tc.tile_pool(name="const", bufs=1))
-        work = ctx.enter_context(tc.tile_pool(name="work", bufs=TILES))
+        per_group = ctx.enter_context(tc.tile_pool(name="per_group", bufs=len(GROUPS)))
+        per_tile = ctx.enter_context(tc.tile_pool(name="per_tile", bufs=TILES))
         psum_const = ctx.enter_context(tc.psum_pool(name="psum_const", bufs=1))
         psum = ctx.enter_context(tc.psum_pool(name="psum", bufs=2))
         ctx.enter_context(tc.manual_schedule())
@@ -43,8 +50,9 @@ def tile_multiheadattention_pa_kernel(
         ident = const.tile([P, P], F32, name="ident")
         row_select = const.tile([P, 2], BF16, name="row_select")
         ab_rows = const.tile([P, D_MODEL], BF16, name="ab_rows")
-        bias_sb = const.tile([P, D_MODEL], BF16, name="bias_sb")
+        gain_sb = const.tile([P, D_MODEL], BF16, name="gain_sb")
         squares = const.tile([P, D_MODEL], F32, name="squares")
+        stats = const.tile([P, TILES, STAT_COLS], F32, name="stats")
         w1_codes = const.tile([P, 2 * D_CONTENT], U8, name="w1_codes", align_bytes=64)
         w2_codes = const.tile([P, 2 * D_POS], U8, name="w2_codes", align_bytes=64)
         w1_scale = const.tile([P, D_CONTENT], U8, name="w1_scale", align_bytes=64)
@@ -52,27 +60,38 @@ def tile_multiheadattention_pa_kernel(
         gain_ps = psum_const.tile([P, D_MODEL], BF16, name="gain_ps")
         bias_ps = psum_const.tile([P, D_MODEL], BF16, name="bias_ps")
 
-        x = [work.tile([P, 2, H, HALF], BF16, name="x") for i in range(TILES)]
-        res = [work.tile([P, D_MODEL], BF16, name="res") for i in range(TILES)]
-        grouped = [work.tile([P, 2 * K], BF16, name="grouped", align_bytes=64) for i in range(TILES)]
-        codes = [work.tile([P, 2 * P], U32, name="codes", align_bytes=64) for i in range(TILES)]
-        scales = [work.tile([P, 2 * P], U8, name="scales", align_bytes=64) for i in range(TILES)]
-        z = [work.tile([P, D_MODEL], F32, name="z") for i in range(TILES)]
-        t = [work.tile([P, D_MODEL], F32, name="t") for i in range(TILES)]
-        stats = [work.tile([P, 8], F32, name="stats") for i in range(TILES)]
-        xt, y_lo, y_hi = {}, {}, {}
+        x = [per_group.tile([P, H, len(g) * D_V], BF16, name="x") for g in GROUPS]
+        grouped = [per_group.tile([P, len(g) * 2 * K], BF16, name="grouped", align_bytes=64) for g in GROUPS]
+        codes = [per_group.tile([P, len(g) * 2 * P], U32, name="codes", align_bytes=64) for g in GROUPS]
+        scales = [per_group.tile([P, len(g) * 2 * P], U8, name="scales", align_bytes=64) for g in GROUPS]
+        words = [per_tile.tile([P, K], F32, name="words") for i in range(TILES)]
+        res = [per_tile.tile([P, D_MODEL], BF16, name="res") for i in range(TILES)]
+        z = [per_tile.tile([P, D_MODEL], F32, name="z") for i in range(TILES)]
+        t = [per_tile.tile([P, D_MODEL], F32, name="t") for i in range(TILES)]
+        xt, y = {}, {}
 
-        def rows(i):
-            return slice(i * P, (i + 1) * P)
+        def place(i):
+            g = group_of[i]
+            return g, i - GROUPS[g][0]
 
-        def stat(i, col):
-            return stats[i][:, col : col + 1]
+        def tile_rows(ap, i):
+            g, r = place(i)
+            n = len(GROUPS[g])
+            first = GROUPS[g][0] * P
+            return ap[first : first + n * P, :].rearrange("(p r) d -> p r d", r=n)[:, r, :]
 
-        def load_half(i, s):
-            nc.sync.dma_start(out=x[i][:, s, :, :], in_=heads[rows(i), :, s * HALF : (s + 1) * HALF])
+        def stat(i, col, n=1):
+            return stats[:, i, col : col + n]
 
-        def load_res(i):
-            nc.sync.dma_start(out=res[i][:], in_=inp[rows(i), :])
+        def load_heads(g):
+            n = len(GROUPS[g])
+            first = GROUPS[g][0] * P
+            nc.sync.dma_start(
+                out=x[g][:], in_=heads[:, first : first + n * P, :].rearrange("h (p r) d -> p h (r d)", r=n)
+            )
+
+        def load_residual(i):
+            nc.sync.dma_start(out=res[i][:], in_=tile_rows(inp, i))
 
         def load_scales(plane, w_scales):
             for q in range(4):
@@ -82,55 +101,61 @@ def tile_multiheadattention_pa_kernel(
                 )
 
         def spread_row(dst, row):
-            for n0 in range(0, D_MODEL, BANK):
+            for cols in (LO, HI):
                 nc.tensor.matmul(
-                    dst[:, n0 : n0 + BANK],
+                    dst[:, cols],
                     lhsT=row_select[:, row : row + 1].to_broadcast([P, P]),
-                    rhs=ab_rows[:, n0 : n0 + BANK],
+                    rhs=ab_rows[:, cols],
                     start=True,
                     stop=True,
                 )
 
-        def transpose(i):
-            xt[i] = psum.tile([P, 4, P], F32, name="xt")
-            words = x[i][:].rearrange("p s h j -> p (s h j)").bitcast(F32)
-            for s in range(2):
-                for u in range(2):
-                    nc.tensor.transpose(xt[i][:, 2 * s + u, :], words[:, 256 * s + u : 256 * (s + 1) : 2], ident[:])
-
-        def interleave(i):
-            nc.scalar.copy(
-                out=grouped[i][:].bitcast(F32).rearrange("p (s r u) -> p s r u", s=2, u=2),
-                in_=xt[i][:].rearrange("p (s u) r -> p s r u", s=2),
+        def regroup(i):
+            g, r = place(i)
+            pairs = x[g][:, :, r * D_V : (r + 1) * D_V].bitcast(F32)
+            nc.vector.tensor_copy(
+                out=words[i][:].rearrange("p (s u h q) -> p s u h q", s=2, u=2, h=H),
+                in_=pairs.rearrange("p h (s q u) -> p s u h q", s=2, u=2),
             )
 
-        def quantize(i):
-            nc.vector.quantize_mx(out=codes[i][:].bitcast(E5M2X4), scales=scales[i][:], in_=grouped[i][:])
+        def transpose(i):
+            g, r = place(i)
+            xt[i] = psum.tile([P, 4, P], F32, name="xt")
+            for j in range(4):
+                nc.tensor.transpose(xt[i][:, j, :], words[i][:, j * P : (j + 1) * P], ident[:])
+            nc.scalar.copy(
+                out=grouped[g][:, r * 2 * K : (r + 1) * 2 * K].bitcast(F32).rearrange("p (s m u) -> p s m u", s=2, u=2),
+                in_=xt[i][:].rearrange("p (s u) m -> p s m u", s=2),
+            )
+
+        def quantize(g):
+            nc.vector.quantize_mx(out=codes[g][:].bitcast(E5M2X4), scales=scales[g][:], in_=grouped[g][:])
 
         def project(i):
-            y_lo[i] = psum.tile([P, BANK], F32, name="y_lo")
-            y_hi[i] = psum.tile([P, BANK], F32, name="y_hi")
+            g, r = place(i)
+            y[i, LO.start] = psum.tile([P, BANK], F32, name="y_lo")
+            y[i, HI.start] = psum.tile([P, BANK], F32, name="y_hi")
             parts = (
-                (y_lo[i][:], 0, w1_codes, w1_scale, 0, BANK),
-                (y_hi[i][:, : D_CONTENT - BANK], 0, w1_codes, w1_scale, BANK, D_CONTENT),
-                (y_hi[i][:, D_CONTENT - BANK :], 1, w2_codes, w2_scale, 0, D_POS),
+                (y[i, LO.start][:], 0, w1_codes, w1_scale, 0, BANK),
+                (y[i, HI.start][:, : D_CONTENT - BANK], 0, w1_codes, w1_scale, BANK, D_CONTENT),
+                (y[i, HI.start][:, D_CONTENT - BANK :], 1, w2_codes, w2_scale, 0, D_POS),
             )
             for dst, s, w_codes, w_scale, n0, n1 in parts:
+                tokens = slice((2 * r + s) * P, (2 * r + s + 1) * P)
                 nc.tensor.matmul_mx(
                     out=dst,
-                    lhsT=codes[i][:, s * P : (s + 1) * P].bitcast(E5M2X4),
-                    lhsT_scale=scales[i][:, s * P : (s + 1) * P],
+                    lhsT=codes[g][:, tokens].bitcast(E5M2X4),
+                    lhsT_scale=scales[g][:, tokens],
                     rhs=w_codes[:, 2 * n0 : 2 * n1].bitcast(E2M1X4),
                     rhs_scale=w_scale[:, n0:n1],
                     start=True,
                     stop=True,
                 )
 
-        def add_residual(i, y, n0, col):
-            cols = slice(n0, n0 + BANK)
+        def add_residual(i, cols, sum_col):
             nc.vector.scalar_tensor_tensor(
-                out=z[i][:, cols], in0=y[:], scalar=1.0, in1=res[i][:, cols],
-                op0=ALU.mult, op1=ALU.add, accum_out=stat(i, col),
+                out=z[i][:, cols], in0=y[i, cols.start][:], scalar=1.0, in1=res[i][:, cols],
+                op0=ALU.mult, op1=ALU.add, accum_out=stat(i, sum_col),
             )
 
         def neg_mean(i):
@@ -139,94 +164,114 @@ def tile_multiheadattention_pa_kernel(
                 op0=ALU.add, op1=ALU.mult,
             )
 
-        def deviation(i):
+        def centre_and_gain(i, cols):
+            nc.scalar.activation(out=t[i][:, cols], in_=z[i][:, cols], func=ACT.Identity, bias=stat(i, NEG_MEAN))
+            nc.gpsimd.tensor_tensor(out=t[i][:, cols], in0=t[i][:, cols], in1=gain_sb[:, cols], op=ALU.mult)
+
+        def centre_and_gain_on_vector(i, cols):
+            nc.vector.scalar_tensor_tensor(
+                out=t[i][:, cols], in0=z[i][:, cols], scalar=stat(i, NEG_MEAN), in1=gain_ps[:, cols],
+                op0=ALU.add, op1=ALU.mult,
+            )
+
+        def sum_of_squares(i):
             nc.scalar.activation(
                 out=squares[:], in_=z[i][:], func=ACT.Square, bias=stat(i, NEG_MEAN), accum_out=stat(i, SUM_SQ)
             )
-            nc.scalar.activation(out=stat(i, SIGMA), in_=stat(i, SUM_SQ), func=ACT.Sqrt, scale=1.0 / (D_MODEL - 1))
-            nc.scalar.activation(out=stat(i, DENOM), in_=stat(i, SIGMA), func=ACT.Copy, bias=EPS)
 
-        def centre_and_gain(i):
-            nc.vector.scalar_tensor_tensor(
-                out=t[i][:], in0=z[i][:], scalar=stat(i, NEG_MEAN), in1=gain_ps[:], op0=ALU.add, op1=ALU.mult
+        def denominator(i):
+            nc.scalar.activation(
+                out=stat(i, ROOTS, 2), in_=stat(i, SUM_SQ, 2), func=ACT.Sqrt, scale=1.0 / (D_MODEL - 1),
+                accum_out=stat(i, DENOM),
             )
 
-        def reciprocal(i):
+        def invert(i):
             nc.vector.reciprocal(out=stat(i, RSTD), in_=stat(i, DENOM))
 
-        def finish(i):
-            nc.scalar.activation(out=t[i][:], in_=t[i][:], func=ACT.Copy, scale=stat(i, RSTD))
-            nc.gpsimd.tensor_tensor(out=t[i][:], in0=t[i][:], in1=bias_sb[:], op=ALU.add)
-            nc.sync.dma_start(out=out[rows(i), :], in_=t[i][:])
-
-        def finish_last(i):
-            for n0 in range(0, D_MODEL, BANK):
-                cols = slice(n0, n0 + BANK)
-                nc.vector.scalar_tensor_tensor(
-                    out=t[i][:, cols], in0=t[i][:, cols], scalar=stat(i, RSTD), in1=bias_ps[:, cols],
-                    op0=ALU.mult, op1=ALU.add,
-                )
-                nc.sync.dma_start(out=out[rows(i), cols], in_=t[i][:, cols])
+        def finish(i, cols):
+            nc.vector.scalar_tensor_tensor(
+                out=t[i][:, cols], in0=t[i][:, cols], scalar=stat(i, RSTD), in1=bias_ps[:, cols],
+                op0=ALU.mult, op1=ALU.add,
+            )
+            nc.sync.dma_start(out=tile_rows(out, i)[:, cols], in_=t[i][:, cols])
 
         nc.vector.memset(w1_scale[:].bitcast(I32), 0)
-        nc.vector.memset(w2_scale[:].bitcast(I32), 0)
         nc.vector.memset(ab_rows[:].bitcast(I32), 0)
-        make_identity(nc, ident[:])
-        nc.scalar.activation(out=row_select[:], in_=ident[:, 0:2], func=ACT.Sqrt)
+        nc.vector.memset(w2_scale[:].bitcast(I32), 0)
+        nc.vector.memset(stats[:, :, EPS_SQ], 1.0)
+        nc.vector.tensor_scalar_mul(stats[:, :, EPS_SQ], stats[:, :, EPS_SQ], (D_MODEL - 1) * EPS * EPS)
 
-        load_half(0, 0)
-        load_half(0, 1)
-        load_scales(w1_scale, w_proj1_scales)
-        load_half(1, 0)
-        load_half(1, 1)
-        load_res(0)
-        load_half(2, 0)
-        load_scales(w2_scale, w_proj2_scales)
-        load_half(2, 1)
-        load_res(1)
-        for i in range(3, TILES):
-            load_half(i, 0)
-            load_half(i, 1)
-            load_res(i - 1)
-        load_res(TILES - 1)
+        make_identity(nc, ident[:])
         nc.gpsimd.dma_start(out=w1_codes[:].bitcast(I32), in_=w_proj1_words[0].bitcast(I32))
-        nc.gpsimd.dma_start(out=w2_codes[:].bitcast(I32), in_=w_proj2_words[0].bitcast(I32))
         nc.gpsimd.dma_start(out=ab_rows[0:1, :], in_=ln_a.rearrange("(o n) -> o n", o=1))
         nc.gpsimd.dma_start(out=ab_rows[1:2, :], in_=ln_b.rearrange("(o n) -> o n", o=1))
+        nc.scalar.activation(out=row_select[:], in_=ident[:, 0:2], func=ACT.Sqrt)
 
+        load_heads(0)
+        load_scales(w1_scale, w_proj1_scales)
+        load_heads(1)
+        load_heads(2)
+        load_residual(0)
+        load_scales(w2_scale, w_proj2_scales)
+        nc.sync.dma_start(out=w2_codes[:].bitcast(I32), in_=w_proj2_words[0].bitcast(I32))
+        load_heads(3)
+        load_heads(4)
+        for i in range(1, TILES):
+            load_residual(i)
+
+        regroup(0)
         transpose(0)
-        interleave(0)
+        regroup(1)
         transpose(1)
-        interleave(1)
         quantize(0)
         project(0)
+        for i in GROUPS[2]:
+            regroup(i)
+            transpose(i)
         quantize(1)
-        transpose(2)
-        interleave(2)
-        project(1)
-        add_residual(0, y_lo[0], 0, SUM_LO)
         spread_row(gain_ps, 0)
+        nc.scalar.copy(out=gain_sb[:], in_=gain_ps[:])
+        project(1)
+        add_residual(0, LO, SUM_LO)
 
-        for i in range(TILES):
-            add_residual(i, y_hi[i], BANK, SUM_HI)
-            if i + 3 < TILES:
-                transpose(i + 3)
+        for i in range(TILES + LAG):
+            done = i - LAG
+            if i < TILES:
+                add_residual(i, HI, SUM_HI)
             if i == 0:
-                spread_row(bias_ps, 1)
+                for j in GROUPS[3]:
+                    regroup(j)
+                    transpose(j)
+                quantize(2)
             if i + 2 < TILES:
-                quantize(i + 2)
                 project(i + 2)
-            neg_mean(i)
-            if i + 1 < TILES:
-                add_residual(i + 1, y_lo[i + 1], 0, SUM_LO)
-            deviation(i)
-            centre_and_gain(i)
-            reciprocal(i)
-            if i + 3 < TILES:
-                interleave(i + 3)
             if i == 0:
-                nc.scalar.copy(out=bias_sb[:], in_=bias_ps[:])
-            if i + 1 < TILES:
-                finish(i)
-            else:
-                finish_last(i)
+                for j in GROUPS[4]:
+                    regroup(j)
+            if i == 1:
+                spread_row(bias_ps, 1)
+            if i == 2:
+                quantize(4)
+            if done >= 0:
+                finish(done, LO)
+            if i < TILES:
+                neg_mean(i)
+                centre_and_gain(i, HI if i == last else ALL)
+            if 0 < i <= TILES:
+                denominator(i - 1)
+            if i == 0:
+                transpose(GROUPS[4][0])
+            if i < TILES:
+                sum_of_squares(i)
+            if i == 0:
+                transpose(GROUPS[4][1])
+            if i < last:
+                add_residual(i + 1, LO, SUM_LO)
+            if i == 0:
+                quantize(3)
+            if 0 <= i - 2 < TILES:
+                invert(i - 2)
+            if done >= 0:
+                finish(done, HI)
+            if i == last:
+                centre_and_gain_on_vector(last, LO)

from contextlib import ExitStack

import concourse.mybir as mybir
from concourse.masks import make_identity

H, D_CONTENT, D_POS, D_V, T = 8, 768, 256, 128, 1024
D_MODEL = D_CONTENT + D_POS
HALF = D_V // 2
K = H * HALF
EPS = 1e-3
FLOPS = 2 * T * K * D_MODEL

P = 128
TILES = T // P
BANK = 512
GROUPS = ((0,), (1,), (2, 3), (4, 5), (6, 7))
LAG = 3

F32 = mybir.dt.float32
BF16 = mybir.dt.bfloat16
I32 = mybir.dt.int32
U32 = mybir.dt.uint32
U8 = mybir.dt.uint8
E5M2X4 = mybir.dt.float8_e5m2_x4
E2M1X4 = mybir.dt.float4_e2m1fn_x4
ALU = mybir.AluOpType
ACT = mybir.ActivationFunctionType

SUM_LO, SUM_HI, NEG_MEAN, SUM_SQ, EPS_SQ, ROOTS, DENOM, RSTD = 0, 1, 2, 3, 4, 5, 7, 8
STAT_COLS = 9
LO, HI, ALL = slice(0, BANK), slice(BANK, D_MODEL), slice(0, D_MODEL)


def tile_multiheadattention_pa_kernel(
    tc, attn_out, inp, w_proj1_words, w_proj1_scales, w_proj2_words, w_proj2_scales, ln_a, ln_b, out
):
    nc = tc.nc
    heads = attn_out.rearrange("h b l d -> h (b l) d")
    group_of = {i: g for g, tiles in enumerate(GROUPS) for i in tiles}
    last = TILES - 1

    with ExitStack() as ctx:
        const = ctx.enter_context(tc.tile_pool(name="const", bufs=1))
        per_group = ctx.enter_context(tc.tile_pool(name="per_group", bufs=len(GROUPS)))
        per_tile = ctx.enter_context(tc.tile_pool(name="per_tile", bufs=TILES))
        psum_const = ctx.enter_context(tc.psum_pool(name="psum_const", bufs=1))
        psum = ctx.enter_context(tc.psum_pool(name="psum", bufs=2))
        ctx.enter_context(tc.manual_schedule())

        ident = const.tile([P, P], F32, name="ident")
        row_select = const.tile([P, 2], BF16, name="row_select")
        ab_rows = const.tile([P, D_MODEL], BF16, name="ab_rows")
        gain_sb = const.tile([P, D_MODEL], BF16, name="gain_sb")
        squares = const.tile([P, D_MODEL], F32, name="squares")
        stats = const.tile([P, TILES, STAT_COLS], F32, name="stats")
        w1_codes = const.tile([P, 2 * D_CONTENT], U8, name="w1_codes", align_bytes=64)
        w2_codes = const.tile([P, 2 * D_POS], U8, name="w2_codes", align_bytes=64)
        w1_scale = const.tile([P, D_CONTENT], U8, name="w1_scale", align_bytes=64)
        w2_scale = const.tile([P, D_POS], U8, name="w2_scale", align_bytes=64)
        gain_ps = psum_const.tile([P, D_MODEL], BF16, name="gain_ps")
        bias_ps = psum_const.tile([P, D_MODEL], BF16, name="bias_ps")

        x = [per_group.tile([P, H, len(g) * D_V], BF16, name="x") for g in GROUPS]
        grouped = [per_group.tile([P, len(g) * 2 * K], BF16, name="grouped", align_bytes=64) for g in GROUPS]
        codes = [per_group.tile([P, len(g) * 2 * P], U32, name="codes", align_bytes=64) for g in GROUPS]
        scales = [per_group.tile([P, len(g) * 2 * P], U8, name="scales", align_bytes=64) for g in GROUPS]
        words = [per_tile.tile([P, K], F32, name="words") for i in range(TILES)]
        res = [per_tile.tile([P, D_MODEL], BF16, name="res") for i in range(TILES)]
        z = [per_tile.tile([P, D_MODEL], F32, name="z") for i in range(TILES)]
        t = [per_tile.tile([P, D_MODEL], F32, name="t") for i in range(TILES)]
        xt, y = {}, {}

        def place(i):
            g = group_of[i]
            return g, i - GROUPS[g][0]

        def tile_rows(ap, i):
            g, r = place(i)
            n = len(GROUPS[g])
            first = GROUPS[g][0] * P
            return ap[first : first + n * P, :].rearrange("(p r) d -> p r d", r=n)[:, r, :]

        def stat(i, col, n=1):
            return stats[:, i, col : col + n]

        def load_heads(g):
            n = len(GROUPS[g])
            first = GROUPS[g][0] * P
            nc.sync.dma_start(
                out=x[g][:], in_=heads[:, first : first + n * P, :].rearrange("h (p r) d -> p h (r d)", r=n)
            )

        def load_residual(i):
            nc.sync.dma_start(out=res[i][:], in_=tile_rows(inp, i))

        def load_scales(plane, w_scales):
            for q in range(4):
                nc.sync.dma_start(
                    out=plane[32 * q : 32 * q + 4, :].bitcast(I32),
                    in_=w_scales[0, 4 * q : 4 * q + 4, :].bitcast(I32),
                )

        def spread_row(dst, row):
            for cols in (LO, HI):
                nc.tensor.matmul(
                    dst[:, cols],
                    lhsT=row_select[:, row : row + 1].to_broadcast([P, P]),
                    rhs=ab_rows[:, cols],
                    start=True,
                    stop=True,
                )

        def regroup(i):
            g, r = place(i)
            pairs = x[g][:, :, r * D_V : (r + 1) * D_V].bitcast(F32)
            nc.vector.tensor_copy(
                out=words[i][:].rearrange("p (s u h q) -> p s u h q", s=2, u=2, h=H),
                in_=pairs.rearrange("p h (s q u) -> p s u h q", s=2, u=2),
            )

        def transpose(i):
            g, r = place(i)
            xt[i] = psum.tile([P, 4, P], F32, name="xt")
            for j in range(4):
                nc.tensor.transpose(xt[i][:, j, :], words[i][:, j * P : (j + 1) * P], ident[:])
            nc.scalar.copy(
                out=grouped[g][:, r * 2 * K : (r + 1) * 2 * K].bitcast(F32).rearrange("p (s m u) -> p s m u", s=2, u=2),
                in_=xt[i][:].rearrange("p (s u) m -> p s m u", s=2),
            )

        def quantize(g):
            nc.vector.quantize_mx(out=codes[g][:].bitcast(E5M2X4), scales=scales[g][:], in_=grouped[g][:])

        def project(i):
            g, r = place(i)
            y[i, LO.start] = psum.tile([P, BANK], F32, name="y_lo")
            y[i, HI.start] = psum.tile([P, BANK], F32, name="y_hi")
            parts = (
                (y[i, LO.start][:], 0, w1_codes, w1_scale, 0, BANK),
                (y[i, HI.start][:, : D_CONTENT - BANK], 0, w1_codes, w1_scale, BANK, D_CONTENT),
                (y[i, HI.start][:, D_CONTENT - BANK :], 1, w2_codes, w2_scale, 0, D_POS),
            )
            for dst, s, w_codes, w_scale, n0, n1 in parts:
                tokens = slice((2 * r + s) * P, (2 * r + s + 1) * P)
                nc.tensor.matmul_mx(
                    out=dst,
                    lhsT=codes[g][:, tokens].bitcast(E5M2X4),
                    lhsT_scale=scales[g][:, tokens],
                    rhs=w_codes[:, 2 * n0 : 2 * n1].bitcast(E2M1X4),
                    rhs_scale=w_scale[:, n0:n1],
                    start=True,
                    stop=True,
                )

        def add_residual(i, cols, sum_col):
            nc.vector.scalar_tensor_tensor(
                out=z[i][:, cols], in0=y[i, cols.start][:], scalar=1.0, in1=res[i][:, cols],
                op0=ALU.mult, op1=ALU.add, accum_out=stat(i, sum_col),
            )

        def neg_mean(i):
            nc.vector.tensor_scalar(
                out=stat(i, NEG_MEAN), in0=stat(i, SUM_LO), scalar1=stat(i, SUM_HI), scalar2=-1.0 / D_MODEL,
                op0=ALU.add, op1=ALU.mult,
            )

        def centre_and_gain(i, cols):
            nc.scalar.activation(out=t[i][:, cols], in_=z[i][:, cols], func=ACT.Identity, bias=stat(i, NEG_MEAN))
            nc.gpsimd.tensor_tensor(out=t[i][:, cols], in0=t[i][:, cols], in1=gain_sb[:, cols], op=ALU.mult)

        def centre_and_gain_on_vector(i, cols):
            nc.vector.scalar_tensor_tensor(
                out=t[i][:, cols], in0=z[i][:, cols], scalar=stat(i, NEG_MEAN), in1=gain_ps[:, cols],
                op0=ALU.add, op1=ALU.mult,
            )

        def sum_of_squares(i):
            nc.scalar.activation(
                out=squares[:], in_=z[i][:], func=ACT.Square, bias=stat(i, NEG_MEAN), accum_out=stat(i, SUM_SQ)
            )

        def denominator(i):
            nc.scalar.activation(
                out=stat(i, ROOTS, 2), in_=stat(i, SUM_SQ, 2), func=ACT.Sqrt, scale=1.0 / (D_MODEL - 1),
                accum_out=stat(i, DENOM),
            )

        def invert(i):
            nc.vector.reciprocal(out=stat(i, RSTD), in_=stat(i, DENOM))

        def finish(i, cols):
            nc.vector.scalar_tensor_tensor(
                out=t[i][:, cols], in0=t[i][:, cols], scalar=stat(i, RSTD), in1=bias_ps[:, cols],
                op0=ALU.mult, op1=ALU.add,
            )
            nc.sync.dma_start(out=tile_rows(out, i)[:, cols], in_=t[i][:, cols])

        nc.vector.memset(w1_scale[:].bitcast(I32), 0)
        nc.vector.memset(ab_rows[:].bitcast(I32), 0)
        nc.vector.memset(w2_scale[:].bitcast(I32), 0)
        nc.vector.memset(stats[:, :, EPS_SQ], 1.0)
        nc.vector.tensor_scalar_mul(stats[:, :, EPS_SQ], stats[:, :, EPS_SQ], (D_MODEL - 1) * EPS * EPS)

        make_identity(nc, ident[:])
        nc.gpsimd.dma_start(out=w1_codes[:].bitcast(I32), in_=w_proj1_words[0].bitcast(I32))
        nc.gpsimd.dma_start(out=ab_rows[0:1, :], in_=ln_a.rearrange("(o n) -> o n", o=1))
        nc.gpsimd.dma_start(out=ab_rows[1:2, :], in_=ln_b.rearrange("(o n) -> o n", o=1))
        nc.scalar.activation(out=row_select[:], in_=ident[:, 0:2], func=ACT.Sqrt)

        load_heads(0)
        load_scales(w1_scale, w_proj1_scales)
        load_heads(1)
        load_heads(2)
        load_residual(0)
        load_scales(w2_scale, w_proj2_scales)
        nc.sync.dma_start(out=w2_codes[:].bitcast(I32), in_=w_proj2_words[0].bitcast(I32))
        load_heads(3)
        load_heads(4)
        for i in range(1, TILES):
            load_residual(i)

        regroup(0)
        transpose(0)
        regroup(1)
        transpose(1)
        quantize(0)
        project(0)
        for i in GROUPS[2]:
            regroup(i)
            transpose(i)
        quantize(1)
        spread_row(gain_ps, 0)
        nc.scalar.copy(out=gain_sb[:], in_=gain_ps[:])
        project(1)
        add_residual(0, LO, SUM_LO)

        for i in range(TILES + LAG):
            done = i - LAG
            if i < TILES:
                add_residual(i, HI, SUM_HI)
            if i == 0:
                for j in GROUPS[3]:
                    regroup(j)
                    transpose(j)
                quantize(2)
            if i + 2 < TILES:
                project(i + 2)
            if i == 0:
                for j in GROUPS[4]:
                    regroup(j)
            if i == 1:
                spread_row(bias_ps, 1)
            if i == 2:
                quantize(4)
            if done >= 0:
                finish(done, LO)
            if i < TILES:
                neg_mean(i)
                centre_and_gain(i, HI if i == last else ALL)
            if 0 < i <= TILES:
                denominator(i - 1)
            if i == 0:
                transpose(GROUPS[4][0])
            if i < TILES:
                sum_of_squares(i)
            if i == 0:
                transpose(GROUPS[4][1])
            if i < last:
                add_residual(i + 1, LO, SUM_LO)
            if i == 0:
                quantize(3)
            if 0 <= i - 2 < TILES:
                invert(i - 2)
            if done >= 0:
                finish(done, HI)
            if i == last:
                centre_and_gain_on_vector(last, LO)
